import numpy as np
import ml_dtypes


def mxq(x, axis, fmt="e4m3"):
    dtype, down = {"e4m3": (ml_dtypes.float8_e4m3fn, 7), "e5m2": (ml_dtypes.float8_e5m2, 14)}[fmt]
    v = np.moveaxis(np.asarray(x, np.float32).astype(ml_dtypes.bfloat16).astype(np.float64), axis, -1)
    blocks = v.reshape(v.shape[:-1] + (-1, 32))
    amax = np.abs(blocks).max(-1, keepdims=True)
    byte = np.maximum(np.where(amax > 0, np.frexp(amax)[1] - 1 + 127, 0) - down, 1)
    scale = np.exp2(byte - 127.0)
    codes = (blocks / scale).astype(np.float32).astype(dtype).astype(np.float64)
    return np.moveaxis((codes * scale).reshape(v.shape), -1, axis)


WIDE = False


def mx_kscale(k):
    if not WIDE:
        return np.ones(k)
    levels = np.array([10, -10, 5, -5, 0])
    if k % 512:
        return np.exp2(np.random.permutation(np.resize(levels, k // 32))).repeat(32)
    a = np.empty((k // 512, 16))
    for p in range(k // 512):
        a[p, :8] = np.random.permutation(np.resize(levels, 8))
        for g in range(8):
            far = levels[np.abs(levels - a[p, g]) >= 10]
            a[p, g + 8] = far[np.random.randint(len(far))]
    return np.exp2(a.ravel()).repeat(32)


BF16 = ml_dtypes.bfloat16


def bf(x):
    return np.asarray(x, np.float32).astype(BF16)


def f64(x):
    return np.asarray(x).astype(np.float64)


B, N, C, H, R, BLK = 8, 1024, 2048, 32, 256, 16


def setup_inputs():
    s, t = mx_kscale(C), mx_kscale(C)
    return {"wv": bf(np.random.standard_normal((B, N, C)) * 0.12),
            "x": bf(np.random.standard_normal((B, N, C)) * t),
            "dw_w": bf(np.random.standard_normal(C) * 6.0 * s),
            "dw_b": bf(np.random.standard_normal(C) * 0.4 * s),
            "pw_w": bf(np.random.standard_normal((C, C)) / np.sqrt(C) * t[:, None] / s[None, :]),
            "pw_b": bf(np.random.standard_normal(C) * 0.3 * t),
            "p_w1": bf(np.random.standard_normal((R, C)) / np.sqrt(C) / t[None, :])}


def reference(wv, x, dw_w, dw_b, pw_w, pw_b, p_w1):
    a = f64(wv) * f64(dw_w) + f64(dw_b)
    dyn = (mxq(a, 2, "e4m3") @ mxq(f64(pw_w), 1, "e4m3").T) + f64(pw_b)
    y = dyn + f64(x)
    return mxq(y, 2, "e4m3") @ mxq(f64(p_w1), 1, "e4m3").T

@@ -1,0 +1,399 @@
+from contextlib import ExitStack
+
+import concourse.mybir as mybir
+from concourse.masks import make_identity
+
+F32 = mybir.dt.float32
+BF16 = mybir.dt.bfloat16
+U32 = mybir.dt.uint32
+U8 = mybir.dt.uint8
+FP8X4 = mybir.dt.float8_e4m3fn_x4
+ACT = mybir.ActivationFunctionType
+ALU = mybir.AluOpType
+
+TOKENS = 8192
+C = 2048
+R = 256
+P = 128
+CH = 512
+NCH = TOKENS // CH
+NG = C // 512
+STEPS = NCH * NG
+
+FLOPS = 2 * TOKENS * C * C + 2 * TOKENS * C * R
+
+
+def tile_dssattention_pa_l_kernel(tc, wv, x, dw_w, dw_b, pw_w, pw_b, p_w1, out):
+    nc = tc.nc
+    wv_f = wv.flatten_outer_dims()
+    x_f = x.flatten_outer_dims()
+    out_f = out.flatten_outer_dims()
+
+    with ExitStack() as ctx:
+        sb = ctx.enter_context(tc.tile_pool(name="sb", bufs=1))
+        ps = ctx.enter_context(tc.psum_pool(name="ps", bufs=1))
+        ctx.enter_context(tc.manual_schedule())
+
+        ident = sb.tile([P, P], F32, name="ident")
+        make_identity(nc, ident[:])
+
+        vec_f = []
+        for vi, vec in enumerate((dw_w, dw_b, pw_b)):
+            vb = sb.tile([P, NG, 4], BF16, name="vecb%d" % vi)
+            nc.scalar.dma_start(out=vb[:], in_=vec.rearrange("(g p t) -> p g t", g=NG, t=4))
+            vf = sb.tile([P, NG * 4], F32, name="vecf%d" % vi)
+            nc.vector.tensor_copy(out=vf[:], in_=vb[:].rearrange("p g t -> p (g t)"))
+            vec_f.append(vf)
+        dww, dwb, pwb = vec_f
+
+        warm = sb.tile([P, 1], F32, name="warm")
+        nc.vector.memset(warm[:], 0.0)
+        warm2 = sb.tile([P, 1], F32, name="warm2")
+        nc.scalar.activation(out=warm2[:], in_=warm[:], func=ACT.Identity)
+
+        w_codes = []
+        w_scales = []
+        for G in range(NG):
+            wc = sb.tile([P, NG, 512], U32, name="wc%d" % G, align_bytes=64)
+            wsc = sb.tile([P, NG, 512], U8, name="wsc%d" % G, align_bytes=64)
+            w_codes.append(wc)
+            w_scales.append(wsc)
+        w1_codes = sb.tile([P, NG, R], U32, name="w1c", align_bytes=64)
+        w1_scales = sb.tile([P, NG, R], U8, name="w1s", align_bytes=64)
+
+        raw_wv = {}
+        raw_x = {}
+        raw_w = {}
+        bank = {}
+        at = {}
+        grp = {}
+        a_codes = {}
+        a_scales = {}
+        xt = {}
+        yt = {}
+        y_codes = {}
+        y_scales = {}
+
+        def new_raw(rows):
+            t = sb.tile([P, rows, C], BF16, name="raw", tag="raw", bufs=5)
+            return t
+
+        def load_wv(c):
+            t = new_raw(4)
+            nc.sync.dma_start(out=t[:], in_=wv_f[CH * c : CH * (c + 1), :].rearrange("(j p) k -> p j k", p=P))
+            raw_wv[c] = t
+
+        def load_x(c):
+            t = new_raw(4)
+            nc.sync.dma_start(out=t[:], in_=x_f[CH * c : CH * (c + 1), :].rearrange("(j p) k -> p j k", p=P))
+            raw_x[c] = t
+
+        def load_w(G):
+            t = new_raw(4)
+            nc.sync.dma_start(out=t[:], in_=pw_w[512 * G : 512 * (G + 1), :].rearrange("(m t) k -> m t k", t=4))
+            raw_w[G] = t
+
+        def load_w1():
+            t = new_raw(2)
+            nc.sync.dma_start(out=t[:], in_=p_w1.rearrange("(j p) k -> p j k", p=P))
+            raw_w["w1"] = t
+
+        def tr(dst, words, j, g, u):
+            nc.tensor.transpose(dst, words[:, j, 256 * g + u : 256 * (g + 1) : 2], ident[:])
+
+        def t_by_u(key, raw, g):
+            words = raw[:].bitcast(F32)
+            tiles = []
+            for u in range(2):
+                b = ps.tile([P, 512], F32, name="tp", tag="tp", bufs=4)
+                for j in range(4):
+                    tr(b[:, P * j : P * (j + 1)], words, j, g, u)
+                tiles.append(b)
+            bank[key] = tiles
+
+        def t_by_half(key, raw, g, halves):
+            words = raw[:].bitcast(F32)
+            tiles = []
+            for h in range(halves):
+                b = ps.tile([P, 2, 256], F32, name="tp", tag="tp", bufs=4)
+                for u in range(2):
+                    for jj in range(2):
+                        tr(b[:, u, P * jj : P * (jj + 1)], words, 2 * h + jj, g, u)
+                tiles.append(b)
+            bank[key] = tiles
+
+        def copy_halves(key, dst, engines):
+            tiles = bank.pop(key)
+            for h, b in enumerate(tiles):
+                o = dst[:, 256 * h : 256 * (h + 1), :]
+                i = b[:].rearrange("p u r -> p r u")
+                if engines[h % len(engines)] == "s":
+                    nc.scalar.copy(out=o, in_=i)
+                else:
+                    nc.vector.tensor_copy(out=o, in_=i)
+
+        def t_wv(i):
+            t_by_u(("wv", i), raw_wv[i // NG], i % NG)
+
+        def affine(i, engines):
+            g = i % NG
+            tiles = bank.pop(("wv", i))
+            a = sb.tile([P, 4, CH], BF16, name="at", tag="at", bufs=3)
+            for u in range(2):
+                bv = tiles[u][:].bitcast(BF16).rearrange("p (r e) -> p r e", e=2)
+                for e in range(2):
+                    t = 2 * u + e
+                    col = 4 * g + t
+                    if engines[u] == "s":
+                        nc.scalar.activation(out=a[:, t, :], in_=bv[:, :, e], func=ACT.Identity,
+                                             bias=dwb[:, col : col + 1], scale=dww[:, col : col + 1])
+                    else:
+                        nc.vector.tensor_scalar(out=a[:, t, :], in0=bv[:, :, e],
+                                                scalar1=dww[:, col : col + 1], scalar2=dwb[:, col : col + 1],
+                                                op0=ALU.mult, op1=ALU.add)
+            at[i] = a
+
+        def new_grp(shape, dtype):
+            g = sb.tile(shape, dtype, name="grp", tag="grp", bufs=4, align_bytes=64)
+            return g
+
+        def ia_s(i):
+            g = new_grp([P, CH, 4], BF16)
+            grp[("a", i)] = g
+            nc.scalar.copy(out=g[:, 0:256, :], in_=at[i][:, :, 0:256].rearrange("p t c -> p c t"))
+
+        def ia_v(i):
+            g = grp[("a", i)]
+            a = at.pop(i)
+            nc.vector.tensor_copy(out=g[:, 256:512, :], in_=a[:, :, 256:512].rearrange("p t c -> p c t"))
+
+        def q_a(i):
+            g = grp.pop(("a", i))
+            cd = sb.tile([P, CH], U32, name="ac", tag="ac", bufs=10, align_bytes=64)
+            sc = sb.tile([P, CH], U8, name="asc", tag="asc", bufs=10, align_bytes=64)
+            nc.vector.quantize_mx(out=cd[:].bitcast(FP8X4), scales=sc[:], in_=g[:].rearrange("p c t -> p (c t)"))
+            a_codes[i] = cd
+            a_scales[i] = sc
+
+        def t_x(i):
+            t_by_half(("x", i), raw_x[i // NG], i % NG, 2)
+
+        def c_x(i):
+            d = sb.tile([P, CH, 2], F32, name="xt", tag="xt", bufs=3)
+            copy_halves(("x", i), d, ("s",))
+            xt[i] = d
+
+        def t_w(G, gk):
+            t_by_half(("w", G, gk), raw_w[G], gk, 2)
+
+        def c_w(G, gk, engines):
+            d = new_grp([P, 512, 2], F32)
+            copy_halves(("w", G, gk), d, engines)
+            grp[("w", G, gk)] = d
+
+        def q_w(G, gk):
+            d = grp.pop(("w", G, gk))
+            nc.vector.quantize_mx(out=w_codes[G][:, gk, :].bitcast(FP8X4), scales=w_scales[G][:, gk, :],
+                                  in_=d[:].rearrange("p c u -> p (c u)").bitcast(BF16))
+
+        def t_w1(G):
+            t_by_half(("w1", G), raw_w["w1"], G, 1)
+
+        def c_w1(G):
+            d = new_grp([P, R, 2], F32)
+            copy_halves(("w1", G), d, ("s",))
+            grp[("w1", G)] = d
+
+        def q_w1(G):
+            d = grp.pop(("w1", G))
+            nc.vector.quantize_mx(out=w1_codes[:, G, :].bitcast(FP8X4), scales=w1_scales[:, G, :],
+                                  in_=d[:].rearrange("p c u -> p (c u)").bitcast(BF16))
+
+        def m1_y(s, t):
+            c = s // NG
+            G = s % NG
+            acc = ps.tile([P, CH], F32, name="s1", tag="s1", bufs=3)
+            cols = slice(P * t, P * (t + 1))
+            for gk in range(NG):
+                nc.tensor.matmul_mx(out=acc[:],
+                                    lhsT=w_codes[G][:, gk, cols].bitcast(FP8X4), lhsT_scale=w_scales[G][:, gk, cols],
+                                    rhs=a_codes[NG * c + gk][:].bitcast(FP8X4), rhs_scale=a_scales[NG * c + gk][:],
+                                    start=(gk == 0), stop=(gk == NG - 1))
+            if t == 0:
+                y = sb.tile([P, 4, CH], BF16, name="yt", tag="yt", bufs=2)
+                yt[s] = y
+            xv = xt[s][:].rearrange("p r u -> p (r u)").bitcast(BF16).rearrange("p (r t) -> p r t", t=4)
+            col = 4 * G + t
+            nc.vector.scalar_tensor_tensor(out=yt[s][:, t, :], in0=acc[:], scalar=pwb[:, col : col + 1],
+                                           in1=xv[:, :, t], op0=ALU.add, op1=ALU.add)
+
+        def i_y(s):
+            g = sb.tile([P, CH, 4], BF16, name="yg", tag="yg", bufs=2, align_bytes=64)
+            y = yt.pop(s)
+            xt.pop(s)
+            nc.vector.tensor_copy(out=g[:], in_=y[:].rearrange("p t c -> p c t"))
+            grp[("y", s)] = g
+
+        def q_y(s):
+            g = grp.pop(("y", s))
+            cd = sb.tile([P, CH], U32, name="yc", tag="yc", bufs=6, align_bytes=64)
+            sc = sb.tile([P, CH], U8, name="ysc", tag="ysc", bufs=6, align_bytes=64)
+            nc.vector.quantize_mx(out=cd[:].bitcast(FP8X4), scales=sc[:], in_=g[:].rearrange("p c t -> p (c t)"))
+            y_codes[s] = cd
+            y_scales[s] = sc
+
+        def m2(c, h, tag, bufs):
+            acc = ps.tile([P, 2, R], F32, name=tag, tag=tag, bufs=bufs)
+            for jj in range(2):
+                cols = slice(P * (2 * h + jj), P * (2 * h + jj + 1))
+                for G in range(NG):
+                    nc.tensor.matmul_mx(out=acc[:, jj, :],
+                                        lhsT=y_codes[NG * c + G][:, cols].bitcast(FP8X4),
+                                        lhsT_scale=y_scales[NG * c + G][:, cols],
+                                        rhs=w1_codes[:, G, :].bitcast(FP8X4), rhs_scale=w1_scales[:, G, :],
+                                        start=(G == 0), stop=(G == NG - 1))
+            bank[("o", c, h)] = acc
+
+        def store(c, h, engine):
+            acc = bank.pop(("o", c, h))
+            ob = sb.tile([P, 2, R], F32, name="ob", tag="ob", bufs=3)
+            dst = out_f[CH * c + 256 * h : CH * c + 256 * (h + 1), :].rearrange("(jj p) r -> p jj r", p=P)
+            if engine == "s":
+                nc.scalar.copy(out=ob[:], in_=acc[:])
+                nc.scalar.dma_start(out=dst, in_=ob[:])
+            else:
+                nc.vector.tensor_copy(out=ob[:], in_=acc[:])
+                nc.sync.dma_start(out=dst, in_=ob[:])
+
+        load_wv(0)
+        load_w(0)
+        load_x(0)
+        load_w(1)
+        load_wv(1)
+
+        for pair in ((0, 1), (2, 3)):
+            for i in pair:
+                t_wv(i)
+            for i in pair:
+                affine(i, ("s", "v"))
+            for i in pair:
+                ia_s(i)
+                ia_v(i)
+            for i in pair:
+                q_a(i)
+        load_w(2)
+        for pair in ((0, 1), (2, 3)):
+            for gk in pair:
+                t_w(0, gk)
+            for gk in pair:
+                c_w(0, gk, ("s", "v"))
+            for gk in pair:
+                q_w(0, gk)
+        load_w(3)
+        t_x(0)
+        c_x(0)
+
+        runs = {}
+        for s in range(STEPS):
+            first = []
+            if s + 1 < STEPS:
+                first.append(("x", s + 1))
+            if s >= 3 and s + 5 < STEPS:
+                first.append(("wv", s + 5))
+            runs[s] = [first]
+        for s in range(3):
+            runs[s][0].append(("wv", s + 4))
+            runs[s].append([("w", s + 1, 0), ("w", s + 1, 1)])
+            runs[s].append([("w", s + 1, 2), ("w", s + 1, 3)])
+        runs[2].append([("wv", 7)])
+        runs[3].append([("w1", 0), ("w1", 1), ("w1", 2), ("w1", 3)])
+
+        v_stage = []
+        pending_q = []
+
+        def do_run(run):
+            for job in run:
+                if job[0] == "x":
+                    t_x(job[1])
+                elif job[0] == "wv":
+                    t_wv(job[1])
+                elif job[0] == "w":
+                    t_w(job[1], job[2])
+                else:
+                    t_w1(job[1])
+            for job in run:
+                if job[0] == "x":
+                    c_x(job[1])
+                elif job[0] == "wv":
+                    affine(job[1], ("s", "s"))
+                    ia_s(job[1])
+                    v_stage.append(job[1])
+                elif job[0] == "w":
+                    c_w(job[1], job[2], ("s",))
+                    pending_q.append(job)
+                else:
+                    c_w1(job[1])
+                    pending_q.append(job)
+
+        def flush_q():
+            while len(pending_q) > 0:
+                job = pending_q.pop(0)
+                if job[0] == "w":
+                    q_w(job[1], job[2])
+                else:
+                    q_w1(job[1])
+
+        for s in range(STEPS):
+            c = s // NG
+            G = s % NG
+            if G == 0 and c >= 1:
+                if c + 2 < NCH:
+                    load_wv(c + 2)
+                if c + 1 < NCH:
+                    load_x(c + 1)
+            if c >= 1 and G == 1:
+                store(c - 1, 0, "s")
+            if c >= 1 and G == 2:
+                store(c - 1, 1, "s")
+            todo = list(v_stage)
+            while len(v_stage) > 0:
+                v_stage.pop()
+            step_runs = runs[s]
+            do_run(step_runs[0])
+            for i in todo:
+                ia_v(i)
+            if s >= 1:
+                i_y(s - 1)
+            for i in todo:
+                q_a(i)
+            if s >= 1:
+                q_y(s - 1)
+            m1_y(s, 0)
+            m1_y(s, 1)
+            if len(step_runs) > 1:
+                do_run(step_runs[1])
+            m1_y(s, 2)
+            flush_q()
+            if len(step_runs) > 2:
+                do_run(step_runs[2])
+            m1_y(s, 3)
+            flush_q()
+            if len(step_runs) > 3:
+                do_run(step_runs[3])
+            if s == 0:
+                load_x(1)
+            if s == 1:
+                load_wv(2)
+            if s == 2:
+                load_w1()
+            if c >= 1 and G == 0:
+                m2(c - 1, 0, "s2", 1)
+            if c >= 1 and G == 1:
+                m2(c - 1, 1, "s2", 1)
+
+        i_y(STEPS - 1)
+        q_y(STEPS - 1)
+        m2(NCH - 1, 0, "s2", 1)
+        m2(NCH - 1, 1, "s1", 3)
+        store(NCH - 1, 0, "s")
+        store(NCH - 1, 1, "v")

@@ -19,6 +19,10 @@ CH = 512
 NCH = TOKENS // CH
 NG = C // 512
 STEPS = NCH * NG
+RAW_BUFS = 10
+SRT_BUFS = 6
+SORT_AHEAD = 2
+FIRST_SORTED_STEP = 5
 
 FLOPS = 2 * TOKENS * C * C + 2 * TOKENS * C * R
 
@@ -61,9 +65,6 @@ def tile_dssattention_pa_l_kernel(tc, wv, x, dw_w, dw_b, pw_w, pw_b, p_w1, out):
         w1_codes = sb.tile([P, NG, R], U32, name="w1c", align_bytes=64)
         w1_scales = sb.tile([P, NG, R], U8, name="w1s", align_bytes=64)
 
-        raw_wv = {}
-        raw_x = {}
-        raw_w = {}
         bank = {}
         at = {}
         grp = {}
@@ -74,53 +75,64 @@ def tile_dssattention_pa_l_kernel(tc, wv, x, dw_w, dw_b, pw_w, pw_b, p_w1, out):
         y_codes = {}
         y_scales = {}
 
-        def new_raw(rows):
-            t = sb.tile([P, rows, C], BF16, name="raw", tag="raw", bufs=5)
-            return t
+        raw = {}
+        srt = {}
 
-        def load_wv(c):
-            t = new_raw(4)
-            nc.sync.dma_start(out=t[:], in_=wv_f[CH * c : CH * (c + 1), :].rearrange("(j p) k -> p j k", p=P))
-            raw_wv[c] = t
+        def load(job):
+            kind = job[0]
+            rows = 2 if kind == "w1" else 4
+            t = sb.tile([P, rows, 512], BF16, name="raw", tag="raw", bufs=RAW_BUFS)
+            if kind == "wv" or kind == "x":
+                src = wv_f if kind == "wv" else x_f
+                c = job[1] // NG
+                g = job[1] % NG
+                view = src[CH * c : CH * (c + 1), 512 * g : 512 * (g + 1)].rearrange("(j p) k -> p j k", p=P)
+            elif kind == "w":
+                view = pw_w[512 * job[1] : 512 * (job[1] + 1), 512 * job[2] : 512 * (job[2] + 1)].rearrange(
+                    "(m t) k -> m t k", t=4)
+            else:
+                view = p_w1[:, 512 * job[1] : 512 * (job[1] + 1)].rearrange("(j p) k -> p j k", p=P)
+            nc.sync.dma_start(out=t[:], in_=view)
+            raw[job] = t
 
-        def load_x(c):
-            t = new_raw(4)
-            nc.sync.dma_start(out=t[:], in_=x_f[CH * c : CH * (c + 1), :].rearrange("(j p) k -> p j k", p=P))
-            raw_x[c] = t
+        def sort_words(job, engine, parts):
+            r = raw[job]
+            if job not in srt:
+                d = sb.tile([P, 4, 2, P], F32, name="srt", tag="srt", bufs=SRT_BUFS, align_bytes=64)
+                srt[job] = d
+            d = srt[job]
+            lo = parts[0]
+            hi = parts[-1] + 1
+            i = r[:, lo:hi, :].bitcast(F32).rearrange("p j (w u) -> p j u w", u=2)
+            if engine == "s":
+                nc.scalar.copy(out=d[:, lo:hi, :, :], in_=i)
+            else:
+                nc.vector.tensor_copy(out=d[:, lo:hi, :, :], in_=i)
 
-        def load_w(G):
-            t = new_raw(4)
-            nc.sync.dma_start(out=t[:], in_=pw_w[512 * G : 512 * (G + 1), :].rearrange("(m t) k -> m t k", t=4))
-            raw_w[G] = t
+        def tr(dst, job, j, u):
+            if job in srt:
+                nc.tensor.transpose(dst, srt[job][:, j, u, :], ident[:])
+            else:
+                nc.tensor.transpose(dst, raw[job][:, j, :].bitcast(F32)[:, u:256:2], ident[:])
 
-        def load_w1():
-            t = new_raw(2)
-            nc.sync.dma_start(out=t[:], in_=p_w1.rearrange("(j p) k -> p j k", p=P))
-            raw_w["w1"] = t
-
-        def tr(dst, words, j, g, u):
-            nc.tensor.transpose(dst, words[:, j, 256 * g + u : 256 * (g + 1) : 2], ident[:])
-
-        def t_by_u(key, raw, g):
-            words = raw[:].bitcast(F32)
+        def t_by_u(job):
             tiles = []
             for u in range(2):
                 b = ps.tile([P, 512], F32, name="tp", tag="tp", bufs=4)
                 for j in range(4):
-                    tr(b[:, P * j : P * (j + 1)], words, j, g, u)
+                    tr(b[:, P * j : P * (j + 1)], job, j, u)
                 tiles.append(b)
-            bank[key] = tiles
+            bank[job] = tiles
 
-        def t_by_half(key, raw, g, halves):
-            words = raw[:].bitcast(F32)
+        def t_by_half(job, halves):
             tiles = []
             for h in range(halves):
                 b = ps.tile([P, 2, 256], F32, name="tp", tag="tp", bufs=4)
                 for u in range(2):
                     for jj in range(2):
-                        tr(b[:, u, P * jj : P * (jj + 1)], words, 2 * h + jj, g, u)
+                        tr(b[:, u, P * jj : P * (jj + 1)], job, 2 * h + jj, u)
                 tiles.append(b)
-            bank[key] = tiles
+            bank[job] = tiles
 
         def copy_halves(key, dst, engines):
             tiles = bank.pop(key)
@@ -133,7 +145,7 @@ def tile_dssattention_pa_l_kernel(tc, wv, x, dw_w, dw_b, pw_w, pw_b, p_w1, out):
                     nc.vector.tensor_copy(out=o, in_=i)
 
         def t_wv(i):
-            t_by_u(("wv", i), raw_wv[i // NG], i % NG)
+            t_by_u(("wv", i))
 
         def affine(i, engines):
             g = i % NG
@@ -154,13 +166,25 @@ def tile_dssattention_pa_l_kernel(tc, wv, x, dw_w, dw_b, pw_w, pw_b, p_w1, out):
             at[i] = a
 
         def new_grp(shape, dtype):
-            g = sb.tile(shape, dtype, name="grp", tag="grp", bufs=4, align_bytes=64)
+            if dtype == BF16:
+                g = sb.tile(shape, dtype, name="ag", tag="ag", bufs=3, align_bytes=64)
+            else:
+                g = sb.tile(shape, dtype, name="srt", tag="srt", bufs=SRT_BUFS, align_bytes=64)
             return g
 
         def ia_s(i):
             g = new_grp([P, CH, 4], BF16)
             grp[("a", i)] = g
             nc.scalar.copy(out=g[:, 0:256, :], in_=at[i][:, :, 0:256].rearrange("p t c -> p c t"))
+
+        def ia_g(i):
+            g = new_grp([P, CH, 4], BF16)
+            grp[("a", i)] = g
+            a = at.pop(i)
+            for q in range(4):
+                cols = slice(P * q, P * (q + 1))
+                nc.gpsimd.tensor_scalar(out=g[:, cols, :], in0=a[:, :, cols].rearrange("p t c -> p c t"),
+                                        scalar1=1.0, scalar2=0.0, op0=ALU.mult, op1=ALU.add)
 
         def ia_v(i):
             g = grp[("a", i)]
@@ -176,15 +200,23 @@ def tile_dssattention_pa_l_kernel(tc, wv, x, dw_w, dw_b, pw_w, pw_b, p_w1, out):
             a_scales[i] = sc
 
         def t_x(i):
-            t_by_half(("x", i), raw_x[i // NG], i % NG, 2)
+            t_by_half(("x", i), 2)
 
-        def c_x(i):
-            d = sb.tile([P, CH, 2], F32, name="xt", tag="xt", bufs=3)
-            copy_halves(("x", i), d, ("s",))
-            xt[i] = d
+        def c_x(i, h, engine):
+            if h == 0:
+                d = sb.tile([P, CH, 2], F32, name="xt", tag="xt", bufs=3)
+                xt[i] = d
+            b = bank[("x", i)][h]
+            if h == 1:
+                bank.pop(("x", i))
+            o = xt[i][:, 256 * h : 256 * (h + 1), :]
+            if engine == "s":
+                nc.scalar.copy(out=o, in_=b[:].rearrange("p u r -> p r u"))
+            else:
+                nc.vector.tensor_copy(out=o, in_=b[:].rearrange("p u r -> p r u"))
 
         def t_w(G, gk):
-            t_by_half(("w", G, gk), raw_w[G], gk, 2)
+            t_by_half(("w", G, gk), 2)
 
         def c_w(G, gk, engines):
             d = new_grp([P, 512, 2], F32)
@@ -197,7 +229,7 @@ def tile_dssattention_pa_l_kernel(tc, wv, x, dw_w, dw_b, pw_w, pw_b, p_w1, out):
                                   in_=d[:].rearrange("p c u -> p (c u)").bitcast(BF16))
 
         def t_w1(G):
-            t_by_half(("w1", G), raw_w["w1"], G, 1)
+            t_by_half(("w1", G), 1)
 
         def c_w1(G):
             d = new_grp([P, R, 2], F32)
@@ -226,6 +258,10 @@ def tile_dssattention_pa_l_kernel(tc, wv, x, dw_w, dw_b, pw_w, pw_b, p_w1, out):
             col = 4 * G + t
             nc.vector.scalar_tensor_tensor(out=yt[s][:, t, :], in0=acc[:], scalar=pwb[:, col : col + 1],
                                            in1=xv[:, :, t], op0=ALU.add, op1=ALU.add)
+            if G == NG - 1 and t == 3:
+                for gk in range(NG):
+                    a_codes.pop(NG * c + gk)
+                    a_scales.pop(NG * c + gk)
 
         def i_y(s):
             g = sb.tile([P, CH, 4], BF16, name="yg", tag="yg", bufs=2, align_bytes=64)
@@ -253,6 +289,10 @@ def tile_dssattention_pa_l_kernel(tc, wv, x, dw_w, dw_b, pw_w, pw_b, p_w1, out):
                                         rhs=w1_codes[:, G, :].bitcast(FP8X4), rhs_scale=w1_scales[:, G, :],
                                         start=(G == 0), stop=(G == NG - 1))
             bank[("o", c, h)] = acc
+            if h == 1:
+                for G in range(NG):
+                    y_codes.pop(NG * c + G)
+                    y_scales.pop(NG * c + G)
 
         def store(c, h, engine):
             acc = bank.pop(("o", c, h))
@@ -265,35 +305,9 @@ def tile_dssattention_pa_l_kernel(tc, wv, x, dw_w, dw_b, pw_w, pw_b, p_w1, out):
                 nc.vector.tensor_copy(out=ob[:], in_=acc[:])
                 nc.sync.dma_start(out=dst, in_=ob[:])
 
-        load_wv(0)
-        load_w(0)
-        load_x(0)
-        load_w(1)
-        load_wv(1)
-
-        for pair in ((0, 1), (2, 3)):
-            for i in pair:
-                t_wv(i)
-            for i in pair:
-                affine(i, ("s", "v"))
-            for i in pair:
-                ia_s(i)
-                ia_v(i)
-            for i in pair:
-                q_a(i)
-        load_w(2)
-        for pair in ((0, 1), (2, 3)):
-            for gk in pair:
-                t_w(0, gk)
-            for gk in pair:
-                c_w(0, gk, ("s", "v"))
-            for gk in pair:
-                q_w(0, gk)
-        load_w(3)
-        t_x(0)
-        c_x(0)
-
         runs = {}
+        runs[-1] = [[("wv", 0), ("w", 0, 0)], [("wv", 1), ("w", 0, 1)], [("wv", 2), ("w", 0, 2)], [("wv", 3), ("w", 0, 3)],
+                    [("x", 0)]]
         for s in range(STEPS):
             first = []
             if s + 1 < STEPS:
@@ -308,26 +322,51 @@ def tile_dssattention_pa_l_kernel(tc, wv, x, dw_w, dw_b, pw_w, pw_b, p_w1, out):
         runs[2].append([("wv", 7)])
         runs[3].append([("w1", 0), ("w1", 1), ("w1", 2), ("w1", 3)])
 
+        order = []
+        for s in range(-1, STEPS):
+            for run in runs[s]:
+                order.extend(run)
+        state = {"loaded": 0, "freed": 0}
+
+        def prefetch():
+            while state["loaded"] < len(order) and state["loaded"] - state["freed"] < RAW_BUFS:
+                load(order[state["loaded"]])
+                state["loaded"] = state["loaded"] + 1
+
+        def free_raw(job):
+            raw.pop(job)
+            state["freed"] = state["freed"] + 1
+
         v_stage = []
         pending_q = []
+        x_half = []
+
+        def do_transposes(run):
+            for job in run:
+                if job[0] == "wv":
+                    t_by_u(job)
+                elif job[0] == "w1":
+                    t_by_half(job, 1)
+                else:
+                    t_by_half(job, 2)
+                if job in srt:
+                    srt.pop(job)
+                else:
+                    free_raw(job)
 
         def do_run(run):
+            do_transposes(run)
             for job in run:
-                if job[0] == "x":
-                    t_x(job[1])
-                elif job[0] == "wv":
-                    t_wv(job[1])
-                elif job[0] == "w":
-                    t_w(job[1], job[2])
-                else:
-                    t_w1(job[1])
-            for job in run:
-                if job[0] == "x":
-                    c_x(job[1])
-                elif job[0] == "wv":
+                if job[0] == "wv":
                     affine(job[1], ("s", "s"))
-                    ia_s(job[1])
+                    ia_g(job[1])
                     v_stage.append(job[1])
+            for job in run:
+                if job[0] == "x":
+                    c_x(job[1], 0, "s")
+                    x_half.append(job[1])
+                elif job[0] == "wv":
+                    continue
                 elif job[0] == "w":
                     c_w(job[1], job[2], ("s",))
                     pending_q.append(job)
@@ -343,14 +382,39 @@ def tile_dssattention_pa_l_kernel(tc, wv, x, dw_w, dw_b, pw_w, pw_b, p_w1, out):
                 else:
                     q_w1(job[1])
 
+        prefetch()
+        for run in runs[-1]:
+            do_transposes(run)
+            prefetch()
+            for job in run:
+                if job[0] == "wv":
+                    affine(job[1], ("s", "v"))
+                elif job[0] == "w":
+                    c_w(job[1], job[2], ("s", "v"))
+                else:
+                    c_x(job[1], 0, "s")
+                    c_x(job[1], 1, "v")
+            for job in run:
+                if job[0] == "wv":
+                    ia_s(job[1])
+                    ia_v(job[1])
+            for job in run:
+                if job[0] == "wv":
+                    q_a(job[1])
+                elif job[0] == "w":
+                    q_w(job[1], job[2])
+
+        def sort_next(s, kind, engine, parts):
+            if s + SORT_AHEAD >= FIRST_SORTED_STEP and s + SORT_AHEAD < STEPS:
+                for job in runs[s + SORT_AHEAD][0]:
+                    if job[0] == kind:
+                        sort_words(job, engine, parts)
+                        if parts[-1] == 3:
+                            free_raw(job)
+
         for s in range(STEPS):
             c = s // NG
             G = s % NG
-            if G == 0 and c >= 1:
-                if c + 2 < NCH:
-                    load_wv(c + 2)
-                if c + 1 < NCH:
-                    load_x(c + 1)
             if c >= 1 and G == 1:
                 store(c - 1, 0, "s")
             if c >= 1 and G == 2:
@@ -360,32 +424,32 @@ def tile_dssattention_pa_l_kernel(tc, wv, x, dw_w, dw_b, pw_w, pw_b, p_w1, out):
                 v_stage.pop()
             step_runs = runs[s]
             do_run(step_runs[0])
-            for i in todo:
-                ia_v(i)
+            sort_next(s, "wv", "s", (0, 1, 2, 3))
+            sort_next(s, "x", "s", (0, 1, 2, 3))
+            prefetch()
             if s >= 1:
                 i_y(s - 1)
             for i in todo:
                 q_a(i)
             if s >= 1:
                 q_y(s - 1)
+            while len(x_half) > 0:
+                c_x(x_half.pop(0), 1, "v")
             m1_y(s, 0)
             m1_y(s, 1)
             if len(step_runs) > 1:
                 do_run(step_runs[1])
+                prefetch()
             m1_y(s, 2)
             flush_q()
             if len(step_runs) > 2:
                 do_run(step_runs[2])
+                prefetch()
             m1_y(s, 3)
             flush_q()
             if len(step_runs) > 3:
                 do_run(step_runs[3])
-            if s == 0:
-                load_x(1)
-            if s == 1:
-                load_wv(2)
-            if s == 2:
-                load_w1()
+                prefetch()
             if c >= 1 and G == 0:
                 m2(c - 1, 0, "s2", 1)
             if c >= 1 and G == 1:

@@ -19,10 +19,11 @@ CH = 512
 NCH = TOKENS // CH
 NG = C // 512
 STEPS = NCH * NG
-RAW_BUFS = 10
-SRT_BUFS = 6
+RAW_BUFS = 12
+SRT_BUFS = 8
 SORT_AHEAD = 2
 FIRST_SORTED_STEP = 5
+LEAD = 6
 
 FLOPS = 2 * TOKENS * C * C + 2 * TOKENS * C * R
 
@@ -65,6 +66,8 @@ def tile_dssattention_pa_l_kernel(tc, wv, x, dw_w, dw_b, pw_w, pw_b, p_w1, out):
         w1_codes = sb.tile([P, NG, R], U32, name="w1c", align_bytes=64)
         w1_scales = sb.tile([P, NG, R], U8, name="w1s", align_bytes=64)
 
+        raw = {}
+        srt = {}
         bank = {}
         at = {}
         grp = {}
@@ -75,8 +78,11 @@ def tile_dssattention_pa_l_kernel(tc, wv, x, dw_w, dw_b, pw_w, pw_b, p_w1, out):
         y_codes = {}
         y_scales = {}
 
-        raw = {}
-        srt = {}
+        def copy(engine, o, i):
+            if engine == "s":
+                nc.scalar.copy(out=o, in_=i)
+            else:
+                nc.vector.tensor_copy(out=o, in_=i)
 
         def load(job):
             kind = job[0]
@@ -95,19 +101,49 @@ def tile_dssattention_pa_l_kernel(tc, wv, x, dw_w, dw_b, pw_w, pw_b, p_w1, out):
             nc.sync.dma_start(out=t[:], in_=view)
             raw[job] = t
 
-        def sort_words(job, engine, parts):
-            r = raw[job]
-            if job not in srt:
-                d = sb.tile([P, 4, 2, P], F32, name="srt", tag="srt", bufs=SRT_BUFS, align_bytes=64)
-                srt[job] = d
-            d = srt[job]
-            lo = parts[0]
-            hi = parts[-1] + 1
-            i = r[:, lo:hi, :].bitcast(F32).rearrange("p j (w u) -> p j u w", u=2)
-            if engine == "s":
-                nc.scalar.copy(out=d[:, lo:hi, :, :], in_=i)
-            else:
-                nc.vector.tensor_copy(out=d[:, lo:hi, :, :], in_=i)
+        runs = {}
+        runs[-1] = [[("wv", 0), ("w", 0, 0)], [("wv", 1), ("w", 0, 1)], [("wv", 2), ("w", 0, 2)], [("wv", 3), ("w", 0, 3)],
+                    [("x", 0)]]
+        for s in range(STEPS):
+            first = []
+            if s + 1 < STEPS:
+                first.append(("x", s + 1))
+            if s >= 3 and s + LEAD < STEPS:
+                first.append(("wv", s + LEAD))
+            runs[s] = [first]
+        runs[0][0].append(("wv", 4))
+        runs[1][0].append(("wv", 6))
+        runs[2][0].append(("wv", 7))
+        for s in range(3):
+            runs[s].append([("w", s + 1, 0), ("w", s + 1, 1)])
+            runs[s].append([("w", s + 1, 2), ("w", s + 1, 3)])
+        runs[0].append([("wv", 5)])
+        runs[2].append([("wv", 8)])
+        runs[4].append([("w1", 0), ("w1", 1), ("w1", 2), ("w1", 3)])
+
+        order = []
+        t_step = {}
+        for s in range(-1, STEPS):
+            for run in runs[s]:
+                order.extend(run)
+                for job in run:
+                    t_step[job] = s
+        state = {"loaded": 0, "freed": 0}
+
+        def prefetch():
+            while state["loaded"] < len(order) and state["loaded"] - state["freed"] < RAW_BUFS:
+                load(order[state["loaded"]])
+                state["loaded"] = state["loaded"] + 1
+
+        def free_raw(job):
+            raw.pop(job)
+            state["freed"] = state["freed"] + 1
+
+        def sort_words(job, engine):
+            d = sb.tile([P, 4, 2, P], F32, name="srt", tag="srt", bufs=SRT_BUFS, align_bytes=64)
+            copy(engine, d[:], raw[job][:].bitcast(F32).rearrange("p j (w u) -> p j u w", u=2))
+            srt[job] = d
+            free_raw(job)
 
         def tr(dst, job, j, u):
             if job in srt:
@@ -115,37 +151,29 @@ def tile_dssattention_pa_l_kernel(tc, wv, x, dw_w, dw_b, pw_w, pw_b, p_w1, out):
             else:
                 nc.tensor.transpose(dst, raw[job][:, j, :].bitcast(F32)[:, u:256:2], ident[:])
 
-        def t_by_u(job):
+        def transposes(job):
             tiles = []
-            for u in range(2):
-                b = ps.tile([P, 512], F32, name="tp", tag="tp", bufs=4)
-                for j in range(4):
-                    tr(b[:, P * j : P * (j + 1)], job, j, u)
-                tiles.append(b)
-            bank[job] = tiles
-
-        def t_by_half(job, halves):
-            tiles = []
-            for h in range(halves):
-                b = ps.tile([P, 2, 256], F32, name="tp", tag="tp", bufs=4)
+            if job[0] == "wv":
                 for u in range(2):
-                    for jj in range(2):
-                        tr(b[:, u, P * jj : P * (jj + 1)], job, 2 * h + jj, u)
-                tiles.append(b)
+                    b = ps.tile([P, 512], F32, name="tp", tag="tp", bufs=4)
+                    for j in range(4):
+                        tr(b[:, P * j : P * (j + 1)], job, j, u)
+                    tiles.append(b)
+            else:
+                for h in range(1 if job[0] == "w1" else 2):
+                    b = ps.tile([P, 2, 256], F32, name="tp", tag="tp", bufs=4)
+                    for u in range(2):
+                        for jj in range(2):
+                            tr(b[:, u, P * jj : P * (jj + 1)], job, 2 * h + jj, u)
+                    tiles.append(b)
             bank[job] = tiles
+            if job in srt:
+                srt.pop(job)
+            else:
+                free_raw(job)
 
-        def copy_halves(key, dst, engines):
-            tiles = bank.pop(key)
-            for h, b in enumerate(tiles):
-                o = dst[:, 256 * h : 256 * (h + 1), :]
-                i = b[:].rearrange("p u r -> p r u")
-                if engines[h % len(engines)] == "s":
-                    nc.scalar.copy(out=o, in_=i)
-                else:
-                    nc.vector.tensor_copy(out=o, in_=i)
-
-        def t_wv(i):
-            t_by_u(("wv", i))
+        def copy_half(job, h, dst, engine):
+            copy(engine, dst[:, 256 * h : 256 * (h + 1), :], bank[job][h][:].rearrange("p u r -> p r u"))
 
         def affine(i, engines):
             g = i % NG
@@ -165,92 +193,69 @@ def tile_dssattention_pa_l_kernel(tc, wv, x, dw_w, dw_b, pw_w, pw_b, p_w1, out):
                                                 op0=ALU.mult, op1=ALU.add)
             at[i] = a
 
-        def new_grp(shape, dtype):
-            if dtype == BF16:
-                g = sb.tile(shape, dtype, name="ag", tag="ag", bufs=3, align_bytes=64)
+        def interleave_a(i, lo, hi, engine):
+            o = grp[i][:, lo:hi, :]
+            a = at[i][:, :, lo:hi].rearrange("p t c -> p c t")
+            if engine == "g":
+                nc.gpsimd.tensor_scalar(out=o, in0=a, scalar1=1.0, scalar2=0.0, op0=ALU.mult, op1=ALU.add)
             else:
-                g = sb.tile(shape, dtype, name="srt", tag="srt", bufs=SRT_BUFS, align_bytes=64)
-            return g
+                copy(engine, o, a)
 
-        def ia_s(i):
-            g = new_grp([P, CH, 4], BF16)
-            grp[("a", i)] = g
-            nc.scalar.copy(out=g[:, 0:256, :], in_=at[i][:, :, 0:256].rearrange("p t c -> p c t"))
+        def new_early_group(i):
+            g = sb.tile([P, CH, 4], BF16, name="ag2", tag="ag2", bufs=3, align_bytes=64)
+            grp[i] = g
 
-        def ia_g(i):
-            g = new_grp([P, CH, 4], BF16)
-            grp[("a", i)] = g
-            a = at.pop(i)
+        def interleave_a_gpsimd(i):
+            g = sb.tile([P, CH, 4], BF16, name="ag", tag="ag", bufs=1, align_bytes=64)
+            grp[i] = g
             for q in range(4):
-                cols = slice(P * q, P * (q + 1))
-                nc.gpsimd.tensor_scalar(out=g[:, cols, :], in0=a[:, :, cols].rearrange("p t c -> p c t"),
-                                        scalar1=1.0, scalar2=0.0, op0=ALU.mult, op1=ALU.add)
-
-        def ia_v(i):
-            g = grp[("a", i)]
-            a = at.pop(i)
-            nc.vector.tensor_copy(out=g[:, 256:512, :], in_=a[:, :, 256:512].rearrange("p t c -> p c t"))
+                interleave_a(i, P * q, P * (q + 1), "g")
+            at.pop(i)
 
         def q_a(i):
-            g = grp.pop(("a", i))
-            cd = sb.tile([P, CH], U32, name="ac", tag="ac", bufs=10, align_bytes=64)
-            sc = sb.tile([P, CH], U8, name="asc", tag="asc", bufs=10, align_bytes=64)
+            g = grp.pop(i)
+            cd = sb.tile([P, CH], U32, name="ac", tag="ac", bufs=9, align_bytes=64)
+            sc = sb.tile([P, CH], U8, name="asc", tag="asc", bufs=9, align_bytes=64)
             nc.vector.quantize_mx(out=cd[:].bitcast(FP8X4), scales=sc[:], in_=g[:].rearrange("p c t -> p (c t)"))
             a_codes[i] = cd
             a_scales[i] = sc
-
-        def t_x(i):
-            t_by_half(("x", i), 2)
 
         def c_x(i, h, engine):
             if h == 0:
                 d = sb.tile([P, CH, 2], F32, name="xt", tag="xt", bufs=3)
                 xt[i] = d
-            b = bank[("x", i)][h]
+            copy_half(("x", i), h, xt[i], engine)
             if h == 1:
                 bank.pop(("x", i))
-            o = xt[i][:, 256 * h : 256 * (h + 1), :]
-            if engine == "s":
-                nc.scalar.copy(out=o, in_=b[:].rearrange("p u r -> p r u"))
+
+        def c_w(job, engines):
+            d = sb.tile([P, R if job[0] == "w1" else 512, 2], F32, name="srt", tag="srt", bufs=SRT_BUFS, align_bytes=64)
+            for h in range(len(bank[job])):
+                copy_half(job, h, d, engines[h])
+            bank.pop(job)
+            grp[job] = d
+
+        def q_w(job):
+            d = grp.pop(job)
+            i = d[:].rearrange("p c u -> p (c u)").bitcast(BF16)
+            if job[0] == "w1":
+                nc.vector.quantize_mx(out=w1_codes[:, job[1], :].bitcast(FP8X4), scales=w1_scales[:, job[1], :], in_=i)
             else:
-                nc.vector.tensor_copy(out=o, in_=b[:].rearrange("p u r -> p r u"))
+                nc.vector.quantize_mx(out=w_codes[job[1]][:, job[2], :].bitcast(FP8X4),
+                                      scales=w_scales[job[1]][:, job[2], :], in_=i)
 
-        def t_w(G, gk):
-            t_by_half(("w", G, gk), 2)
-
-        def c_w(G, gk, engines):
-            d = new_grp([P, 512, 2], F32)
-            copy_halves(("w", G, gk), d, engines)
-            grp[("w", G, gk)] = d
-
-        def q_w(G, gk):
-            d = grp.pop(("w", G, gk))
-            nc.vector.quantize_mx(out=w_codes[G][:, gk, :].bitcast(FP8X4), scales=w_scales[G][:, gk, :],
-                                  in_=d[:].rearrange("p c u -> p (c u)").bitcast(BF16))
-
-        def t_w1(G):
-            t_by_half(("w1", G), 1)
-
-        def c_w1(G):
-            d = new_grp([P, R, 2], F32)
-            copy_halves(("w1", G), d, ("s",))
-            grp[("w1", G)] = d
-
-        def q_w1(G):
-            d = grp.pop(("w1", G))
-            nc.vector.quantize_mx(out=w1_codes[:, G, :].bitcast(FP8X4), scales=w1_scales[:, G, :],
-                                  in_=d[:].rearrange("p c u -> p (c u)").bitcast(BF16))
-
-        def m1_y(s, t):
+        def m1_pass(acc, s, t, gk):
             c = s // NG
             G = s % NG
-            acc = ps.tile([P, CH], F32, name="s1", tag="s1", bufs=3)
             cols = slice(P * t, P * (t + 1))
-            for gk in range(NG):
-                nc.tensor.matmul_mx(out=acc[:],
-                                    lhsT=w_codes[G][:, gk, cols].bitcast(FP8X4), lhsT_scale=w_scales[G][:, gk, cols],
-                                    rhs=a_codes[NG * c + gk][:].bitcast(FP8X4), rhs_scale=a_scales[NG * c + gk][:],
-                                    start=(gk == 0), stop=(gk == NG - 1))
+            nc.tensor.matmul_mx(out=acc[:],
+                                lhsT=w_codes[G][:, gk, cols].bitcast(FP8X4), lhsT_scale=w_scales[G][:, gk, cols],
+                                rhs=a_codes[NG * c + gk][:].bitcast(FP8X4), rhs_scale=a_scales[NG * c + gk][:],
+                                start=(gk == 0), stop=(gk == NG - 1))
+
+        def y_add(acc, s, t):
+            c = s // NG
+            G = s % NG
             if t == 0:
                 y = sb.tile([P, 4, CH], BF16, name="yt", tag="yt", bufs=2)
                 yt[s] = y
@@ -258,206 +263,191 @@ def tile_dssattention_pa_l_kernel(tc, wv, x, dw_w, dw_b, pw_w, pw_b, p_w1, out):
             col = 4 * G + t
             nc.vector.scalar_tensor_tensor(out=yt[s][:, t, :], in0=acc[:], scalar=pwb[:, col : col + 1],
                                            in1=xv[:, :, t], op0=ALU.add, op1=ALU.add)
-            if G == NG - 1 and t == 3:
-                for gk in range(NG):
-                    a_codes.pop(NG * c + gk)
-                    a_scales.pop(NG * c + gk)
+            if t == 3:
+                xt.pop(s)
+                if G == NG - 1:
+                    for gk in range(NG):
+                        a_codes.pop(NG * c + gk)
+                        a_scales.pop(NG * c + gk)
 
-        def i_y(s):
-            g = sb.tile([P, CH, 4], BF16, name="yg", tag="yg", bufs=2, align_bytes=64)
-            y = yt.pop(s)
-            xt.pop(s)
-            nc.vector.tensor_copy(out=g[:], in_=y[:].rearrange("p t c -> p c t"))
-            grp[("y", s)] = g
+        def m1_y(s, t):
+            acc = ps.tile([P, CH], F32, name="s1", tag="s1", bufs=4)
+            for gk in range(NG):
+                m1_pass(acc, s, t, gk)
+            y_add(acc, s, t)
 
-        def q_y(s):
-            g = grp.pop(("y", s))
-            cd = sb.tile([P, CH], U32, name="yc", tag="yc", bufs=6, align_bytes=64)
-            sc = sb.tile([P, CH], U8, name="ysc", tag="ysc", bufs=6, align_bytes=64)
-            nc.vector.quantize_mx(out=cd[:].bitcast(FP8X4), scales=sc[:], in_=g[:].rearrange("p c t -> p (c t)"))
-            y_codes[s] = cd
-            y_scales[s] = sc
+        def i_y(s, lo, hi):
+            if lo == 0:
+                g = sb.tile([P, CH, 4], BF16, name="yg", tag="yg", bufs=2, align_bytes=64)
+                grp[("y", s)] = g
+            nc.vector.tensor_copy(out=grp[("y", s)][:, lo:hi, :], in_=yt[s][:, :, lo:hi].rearrange("p t c -> p c t"))
+            if hi == CH:
+                yt.pop(s)
 
-        def m2(c, h, tag, bufs):
-            acc = ps.tile([P, 2, R], F32, name=tag, tag=tag, bufs=bufs)
+        def q_y(s, lo, hi):
+            if lo == 0:
+                cd = sb.tile([P, CH], U32, name="yc", tag="yc", bufs=6, align_bytes=64)
+                sc = sb.tile([P, CH], U8, name="ysc", tag="ysc", bufs=6, align_bytes=64)
+                y_codes[s] = cd
+                y_scales[s] = sc
+            nc.vector.quantize_mx(out=y_codes[s][:, lo:hi].bitcast(FP8X4), scales=y_scales[s][:, lo:hi],
+                                  in_=grp[("y", s)][:, lo:hi, :].rearrange("p c t -> p (c t)"))
+            if hi == CH:
+                grp.pop(("y", s))
+
+        def m2_pass(acc, c, j, G):
+            cols = slice(P * j, P * (j + 1))
+            nc.tensor.matmul_mx(out=acc,
+                                lhsT=y_codes[NG * c + G][:, cols].bitcast(FP8X4),
+                                lhsT_scale=y_scales[NG * c + G][:, cols],
+                                rhs=w1_codes[:, G, :].bitcast(FP8X4), rhs_scale=w1_scales[:, G, :],
+                                start=(G == 0), stop=(G == NG - 1))
+
+        def m2(c, h):
+            acc = ps.tile([P, 2, R], F32, name="s1", tag="s1", bufs=4)
             for jj in range(2):
-                cols = slice(P * (2 * h + jj), P * (2 * h + jj + 1))
                 for G in range(NG):
-                    nc.tensor.matmul_mx(out=acc[:, jj, :],
-                                        lhsT=y_codes[NG * c + G][:, cols].bitcast(FP8X4),
-                                        lhsT_scale=y_scales[NG * c + G][:, cols],
-                                        rhs=w1_codes[:, G, :].bitcast(FP8X4), rhs_scale=w1_scales[:, G, :],
-                                        start=(G == 0), stop=(G == NG - 1))
+                    m2_pass(acc[:, jj, :], c, 2 * h + jj, G)
             bank[("o", c, h)] = acc
             if h == 1:
                 for G in range(NG):
                     y_codes.pop(NG * c + G)
                     y_scales.pop(NG * c + G)
 
-        def store(c, h, engine):
+        def out_rows(c, h):
+            return out_f[CH * c + 256 * h : CH * c + 256 * (h + 1), :].rearrange("(jj p) r -> p jj r", p=P)
+
+        def store(c, h):
             acc = bank.pop(("o", c, h))
             ob = sb.tile([P, 2, R], F32, name="ob", tag="ob", bufs=3)
-            dst = out_f[CH * c + 256 * h : CH * c + 256 * (h + 1), :].rearrange("(jj p) r -> p jj r", p=P)
-            if engine == "s":
-                nc.scalar.copy(out=ob[:], in_=acc[:])
-                nc.scalar.dma_start(out=dst, in_=ob[:])
+            nc.scalar.copy(out=ob[:], in_=acc[:])
+            nc.scalar.dma_start(out=out_rows(c, h), in_=ob[:])
+
+        prefetch()
+        acc0 = []
+        for t in range(4):
+            acc0.append(ps.tile([P, CH], F32, name="s1", tag="s1", bufs=4))
+        for i in range(NG):
+            transposes(("wv", i))
+            transposes(("w", 0, i))
+            prefetch()
+            affine(i, ("s", "v"))
+            c_w(("w", 0, i), ("s", "v"))
+            new_early_group(i)
+            interleave_a(i, 0, 256, "s")
+            interleave_a(i, 256, 384, "g")
+            interleave_a(i, 384, 512, "g")
+            at.pop(i)
+            if i >= 2:
+                for t in range(4):
+                    m1_pass(acc0[t], 0, t, i - 2)
+            q_w(("w", 0, i))
+            if i >= 1:
+                q_a(i - 1)
+        transposes(("x", 0))
+        prefetch()
+        for t in range(4):
+            m1_pass(acc0[t], 0, t, NG - 2)
+        c_x(0, 0, "s")
+        q_a(NG - 1)
+        c_x(0, 1, "v")
+        for t in range(4):
+            m1_pass(acc0[t], 0, t, NG - 1)
+
+        early_q = {}
+        gpsimd_ia = {}
+        steady_q = {}
+        for i in range(NG, STEPS):
+            ts = t_step[("wv", i)]
+            if i < 8:
+                early_q[ts + 1] = early_q.get(ts + 1, []) + [i]
             else:
-                nc.vector.tensor_copy(out=ob[:], in_=acc[:])
-                nc.sync.dma_start(out=dst, in_=ob[:])
+                gpsimd_ia[ts + 1] = gpsimd_ia.get(ts + 1, []) + [i]
+                steady_q[ts + 2] = steady_q.get(ts + 2, []) + [i]
 
-        runs = {}
-        runs[-1] = [[("wv", 0), ("w", 0, 0)], [("wv", 1), ("w", 0, 1)], [("wv", 2), ("w", 0, 2)], [("wv", 3), ("w", 0, 3)],
-                    [("x", 0)]]
-        for s in range(STEPS):
-            first = []
-            if s + 1 < STEPS:
-                first.append(("x", s + 1))
-            if s >= 3 and s + 5 < STEPS:
-                first.append(("wv", s + 5))
-            runs[s] = [first]
-        for s in range(3):
-            runs[s][0].append(("wv", s + 4))
-            runs[s].append([("w", s + 1, 0), ("w", s + 1, 1)])
-            runs[s].append([("w", s + 1, 2), ("w", s + 1, 3)])
-        runs[2].append([("wv", 7)])
-        runs[3].append([("w1", 0), ("w1", 1), ("w1", 2), ("w1", 3)])
-
-        order = []
-        for s in range(-1, STEPS):
-            for run in runs[s]:
-                order.extend(run)
-        state = {"loaded": 0, "freed": 0}
-
-        def prefetch():
-            while state["loaded"] < len(order) and state["loaded"] - state["freed"] < RAW_BUFS:
-                load(order[state["loaded"]])
-                state["loaded"] = state["loaded"] + 1
-
-        def free_raw(job):
-            raw.pop(job)
-            state["freed"] = state["freed"] + 1
-
-        v_stage = []
         pending_q = []
-        x_half = []
 
-        def do_transposes(run):
+        def do_run(run, extra):
             for job in run:
-                if job[0] == "wv":
-                    t_by_u(job)
-                elif job[0] == "w1":
-                    t_by_half(job, 1)
-                else:
-                    t_by_half(job, 2)
-                if job in srt:
-                    srt.pop(job)
-                else:
-                    free_raw(job)
-
-        def do_run(run):
-            do_transposes(run)
-            for job in run:
-                if job[0] == "wv":
-                    affine(job[1], ("s", "s"))
-                    ia_g(job[1])
-                    v_stage.append(job[1])
+                transposes(job)
+            prefetch()
             for job in run:
                 if job[0] == "x":
                     c_x(job[1], 0, "s")
-                    x_half.append(job[1])
-                elif job[0] == "wv":
-                    continue
-                elif job[0] == "w":
-                    c_w(job[1], job[2], ("s",))
-                    pending_q.append(job)
-                else:
-                    c_w1(job[1])
+            for job in run:
+                if job[0] == "wv":
+                    affine(job[1], ("s", "v") if extra else ("s", "s"))
+                    if job[1] < 8:
+                        new_early_group(job[1])
+                        interleave_a(job[1], 0, 256, "s")
+                elif job[0] == "w" or job[0] == "w1":
+                    c_w(job, ("s", "v") if t_step[job] == 0 else ("s", "s"))
                     pending_q.append(job)
 
         def flush_q():
             while len(pending_q) > 0:
-                job = pending_q.pop(0)
-                if job[0] == "w":
-                    q_w(job[1], job[2])
-                else:
-                    q_w1(job[1])
-
-        prefetch()
-        for run in runs[-1]:
-            do_transposes(run)
-            prefetch()
-            for job in run:
-                if job[0] == "wv":
-                    affine(job[1], ("s", "v"))
-                elif job[0] == "w":
-                    c_w(job[1], job[2], ("s", "v"))
-                else:
-                    c_x(job[1], 0, "s")
-                    c_x(job[1], 1, "v")
-            for job in run:
-                if job[0] == "wv":
-                    ia_s(job[1])
-                    ia_v(job[1])
-            for job in run:
-                if job[0] == "wv":
-                    q_a(job[1])
-                elif job[0] == "w":
-                    q_w(job[1], job[2])
-
-        def sort_next(s, kind, engine, parts):
-            if s + SORT_AHEAD >= FIRST_SORTED_STEP and s + SORT_AHEAD < STEPS:
-                for job in runs[s + SORT_AHEAD][0]:
-                    if job[0] == kind:
-                        sort_words(job, engine, parts)
-                        if parts[-1] == 3:
-                            free_raw(job)
+                q_w(pending_q.pop(0))
 
         for s in range(STEPS):
             c = s // NG
             G = s % NG
             if c >= 1 and G == 1:
-                store(c - 1, 0, "s")
+                store(c - 1, 0)
             if c >= 1 and G == 2:
-                store(c - 1, 1, "s")
-            todo = list(v_stage)
-            while len(v_stage) > 0:
-                v_stage.pop()
+                store(c - 1, 1)
             step_runs = runs[s]
-            do_run(step_runs[0])
-            sort_next(s, "wv", "s", (0, 1, 2, 3))
-            sort_next(s, "x", "s", (0, 1, 2, 3))
-            prefetch()
+            do_run(step_runs[0], False)
+            if s + SORT_AHEAD >= FIRST_SORTED_STEP and s + SORT_AHEAD < STEPS:
+                for job in reversed(runs[s + SORT_AHEAD][0]):
+                    sort_words(job, "s")
+                prefetch()
             if s >= 1:
-                i_y(s - 1)
-            for i in todo:
+                i_y(s - 1, 0, CH)
+            if s + 1 < STEPS:
+                c_x(s + 1, 1, "v")
+            if s >= 1:
+                q_y(s - 1, 0, CH)
+            for i in early_q.get(s, []):
+                interleave_a(i, 256, 512, "v")
+                at.pop(i)
+            for i in early_q.get(s, []):
                 q_a(i)
-            if s >= 1:
-                q_y(s - 1)
-            while len(x_half) > 0:
-                c_x(x_half.pop(0), 1, "v")
-            m1_y(s, 0)
-            m1_y(s, 1)
-            if len(step_runs) > 1:
-                do_run(step_runs[1])
-                prefetch()
-            m1_y(s, 2)
-            flush_q()
-            if len(step_runs) > 2:
-                do_run(step_runs[2])
-                prefetch()
-            m1_y(s, 3)
-            flush_q()
-            if len(step_runs) > 3:
-                do_run(step_runs[3])
-                prefetch()
+            for i in steady_q.get(s, []):
+                q_a(i)
+            for i in gpsimd_ia.get(s, []):
+                interleave_a_gpsimd(i)
+            for t in range(4):
+                if s == 0:
+                    y_add(acc0[t], 0, t)
+                else:
+                    m1_y(s, t)
+                if t >= 2:
+                    flush_q()
+                if t >= 1 and len(step_runs) > t:
+                    do_run(step_runs[t], t == 3)
+            if s == 0:
+                while len(acc0) > 0:
+                    acc0.pop()
             if c >= 1 and G == 0:
-                m2(c - 1, 0, "s2", 1)
+                m2(c - 1, 0)
             if c >= 1 and G == 1:
-                m2(c - 1, 1, "s2", 1)
+                m2(c - 1, 1)
 
-        i_y(STEPS - 1)
-        q_y(STEPS - 1)
-        m2(NCH - 1, 0, "s2", 1)
-        m2(NCH - 1, 1, "s1", 3)
-        store(NCH - 1, 0, "s")
-        store(NCH - 1, 1, "v")
+        c = NCH - 1
+        accs = []
+        for j in range(4):
+            accs.append(ps.tile([P, R], F32, name="tp", tag="tp", bufs=4))
+            for G in range(NG - 1):
+                m2_pass(accs[j][:], c, j, G)
+        for h in range(2):
+            i_y(STEPS - 1, 256 * h, 256 * (h + 1))
+            q_y(STEPS - 1, 256 * h, 256 * (h + 1))
+        for h in range(2):
+            ob = sb.tile([P, 2, R], F32, name="ob", tag="ob", bufs=3)
+            for jj in range(2):
+                m2_pass(accs[2 * h + jj][:], c, 2 * h + jj, NG - 1)
+                copy("s" if h == 0 else "v", ob[:, jj, :], accs[2 * h + jj][:])
+            if h == 0:
+                nc.scalar.dma_start(out=out_rows(c, h), in_=ob[:])
+            else:
+                nc.sync.dma_start(out=out_rows(c, h), in_=ob[:])

@@ -59,12 +59,12 @@ def tile_dssattention_pa_l_kernel(tc, wv, x, dw_w, dw_b, pw_w, pw_b, p_w1, out):
         w_codes = []
         w_scales = []
         for G in range(NG):
-            wc = sb.tile([P, NG, 512], U32, name="wc%d" % G, align_bytes=64)
-            wsc = sb.tile([P, NG, 512], U8, name="wsc%d" % G, align_bytes=64)
+            wc = sb.tile([P, NG, 512], U32, name="wc%d" % G, align_bytes=256)
+            wsc = sb.tile([P, NG, 512], U8, name="wsc%d" % G, align_bytes=256)
             w_codes.append(wc)
             w_scales.append(wsc)
-        w1_codes = sb.tile([P, NG, R], U32, name="w1c", align_bytes=64)
-        w1_scales = sb.tile([P, NG, R], U8, name="w1s", align_bytes=64)
+        w1_codes = sb.tile([P, NG, R], U32, name="w1c", align_bytes=256)
+        w1_scales = sb.tile([P, NG, R], U8, name="w1s", align_bytes=256)
 
         raw = {}
         srt = {}
@@ -214,8 +214,8 @@ def tile_dssattention_pa_l_kernel(tc, wv, x, dw_w, dw_b, pw_w, pw_b, p_w1, out):
 
         def q_a(i):
             g = grp.pop(i)
-            cd = sb.tile([P, CH], U32, name="ac", tag="ac", bufs=9, align_bytes=64)
-            sc = sb.tile([P, CH], U8, name="asc", tag="asc", bufs=9, align_bytes=64)
+            cd = sb.tile([P, CH], U32, name="ac", tag="ac", bufs=9, align_bytes=256)
+            sc = sb.tile([P, CH], U8, name="asc", tag="asc", bufs=9, align_bytes=256)
             nc.vector.quantize_mx(out=cd[:].bitcast(FP8X4), scales=sc[:], in_=g[:].rearrange("p c t -> p (c t)"))
             a_codes[i] = cd
             a_scales[i] = sc
@@ -286,8 +286,8 @@ def tile_dssattention_pa_l_kernel(tc, wv, x, dw_w, dw_b, pw_w, pw_b, p_w1, out):
 
         def q_y(s, lo, hi):
             if lo == 0:
-                cd = sb.tile([P, CH], U32, name="yc", tag="yc", bufs=6, align_bytes=64)
-                sc = sb.tile([P, CH], U8, name="ysc", tag="ysc", bufs=6, align_bytes=64)
+                cd = sb.tile([P, CH], U32, name="yc", tag="yc", bufs=6, align_bytes=256)
+                sc = sb.tile([P, CH], U8, name="ysc", tag="ysc", bufs=6, align_bytes=256)
                 y_codes[s] = cd
                 y_scales[s] = sc
             nc.vector.quantize_mx(out=y_codes[s][:, lo:hi].bitcast(FP8X4), scales=y_scales[s][:, lo:hi],

from contextlib import ExitStack

import concourse.mybir as mybir
from concourse.masks import make_identity

F32 = mybir.dt.float32
BF16 = mybir.dt.bfloat16
U32 = mybir.dt.uint32
U8 = mybir.dt.uint8
FP8X4 = mybir.dt.float8_e4m3fn_x4
ACT = mybir.ActivationFunctionType
ALU = mybir.AluOpType

TOKENS = 8192
C = 2048
R = 256
P = 128
CH = 512
NCH = TOKENS // CH
NG = C // 512
STEPS = NCH * NG
RAW_BUFS = 12
SRT_BUFS = 8
SORT_AHEAD = 2
FIRST_SORTED_STEP = 5
LEAD = 6

FLOPS = 2 * TOKENS * C * C + 2 * TOKENS * C * R


def tile_dssattention_pa_l_kernel(tc, wv, x, dw_w, dw_b, pw_w, pw_b, p_w1, out):
    nc = tc.nc
    wv_f = wv.flatten_outer_dims()
    x_f = x.flatten_outer_dims()
    out_f = out.flatten_outer_dims()

    with ExitStack() as ctx:
        sb = ctx.enter_context(tc.tile_pool(name="sb", bufs=1))
        ps = ctx.enter_context(tc.psum_pool(name="ps", bufs=1))
        ctx.enter_context(tc.manual_schedule())

        ident = sb.tile([P, P], F32, name="ident")
        make_identity(nc, ident[:])

        vec_f = []
        for vi, vec in enumerate((dw_w, dw_b, pw_b)):
            vb = sb.tile([P, NG, 4], BF16, name="vecb%d" % vi)
            nc.scalar.dma_start(out=vb[:], in_=vec.rearrange("(g p t) -> p g t", g=NG, t=4))
            vf = sb.tile([P, NG * 4], F32, name="vecf%d" % vi)
            nc.vector.tensor_copy(out=vf[:], in_=vb[:].rearrange("p g t -> p (g t)"))
            vec_f.append(vf)
        dww, dwb, pwb = vec_f

        warm = sb.tile([P, 1], F32, name="warm")
        nc.vector.memset(warm[:], 0.0)
        warm2 = sb.tile([P, 1], F32, name="warm2")
        nc.scalar.activation(out=warm2[:], in_=warm[:], func=ACT.Identity)

        w_codes = []
        w_scales = []
        for G in range(NG):
            wc = sb.tile([P, NG, 512], U32, name="wc%d" % G, align_bytes=256)
            wsc = sb.tile([P, NG, 512], U8, name="wsc%d" % G, align_bytes=256)
            w_codes.append(wc)
            w_scales.append(wsc)
        w1_codes = sb.tile([P, NG, R], U32, name="w1c", align_bytes=256)
        w1_scales = sb.tile([P, NG, R], U8, name="w1s", align_bytes=256)

        raw = {}
        srt = {}
        bank = {}
        at = {}
        grp = {}
        a_codes = {}
        a_scales = {}
        xt = {}
        yt = {}
        y_codes = {}
        y_scales = {}

        def copy(engine, o, i):
            if engine == "s":
                nc.scalar.copy(out=o, in_=i)
            else:
                nc.vector.tensor_copy(out=o, in_=i)

        def load(job):
            kind = job[0]
            rows = 2 if kind == "w1" else 4
            t = sb.tile([P, rows, 512], BF16, name="raw", tag="raw", bufs=RAW_BUFS)
            if kind == "wv" or kind == "x":
                src = wv_f if kind == "wv" else x_f
                c = job[1] // NG
                g = job[1] % NG
                view = src[CH * c : CH * (c + 1), 512 * g : 512 * (g + 1)].rearrange("(j p) k -> p j k", p=P)
            elif kind == "w":
                view = pw_w[512 * job[1] : 512 * (job[1] + 1), 512 * job[2] : 512 * (job[2] + 1)].rearrange(
                    "(m t) k -> m t k", t=4)
            else:
                view = p_w1[:, 512 * job[1] : 512 * (job[1] + 1)].rearrange("(j p) k -> p j k", p=P)
            nc.sync.dma_start(out=t[:], in_=view)
            raw[job] = t

        runs = {}
        runs[-1] = [[("wv", 0), ("w", 0, 0)], [("wv", 1), ("w", 0, 1)], [("wv", 2), ("w", 0, 2)], [("wv", 3), ("w", 0, 3)],
                    [("x", 0)]]
        for s in range(STEPS):
            first = []
            if s + 1 < STEPS:
                first.append(("x", s + 1))
            if s >= 3 and s + LEAD < STEPS:
                first.append(("wv", s + LEAD))
            runs[s] = [first]
        runs[0][0].append(("wv", 4))
        runs[1][0].append(("wv", 6))
        runs[2][0].append(("wv", 7))
        for s in range(3):
            runs[s].append([("w", s + 1, 0), ("w", s + 1, 1)])
            runs[s].append([("w", s + 1, 2), ("w", s + 1, 3)])
        runs[0].append([("wv", 5)])
        runs[2].append([("wv", 8)])
        runs[4].append([("w1", 0), ("w1", 1), ("w1", 2), ("w1", 3)])

        order = []
        t_step = {}
        for s in range(-1, STEPS):
            for run in runs[s]:
                order.extend(run)
                for job in run:
                    t_step[job] = s
        state = {"loaded": 0, "freed": 0}

        def prefetch():
            while state["loaded"] < len(order) and state["loaded"] - state["freed"] < RAW_BUFS:
                load(order[state["loaded"]])
                state["loaded"] = state["loaded"] + 1

        def free_raw(job):
            raw.pop(job)
            state["freed"] = state["freed"] + 1

        def sort_words(job, engine):
            d = sb.tile([P, 4, 2, P], F32, name="srt", tag="srt", bufs=SRT_BUFS, align_bytes=64)
            copy(engine, d[:], raw[job][:].bitcast(F32).rearrange("p j (w u) -> p j u w", u=2))
            srt[job] = d
            free_raw(job)

        def tr(dst, job, j, u):
            if job in srt:
                nc.tensor.transpose(dst, srt[job][:, j, u, :], ident[:])
            else:
                nc.tensor.transpose(dst, raw[job][:, j, :].bitcast(F32)[:, u:256:2], ident[:])

        def transposes(job):
            tiles = []
            if job[0] == "wv":
                for u in range(2):
                    b = ps.tile([P, 512], F32, name="tp", tag="tp", bufs=4)
                    for j in range(4):
                        tr(b[:, P * j : P * (j + 1)], job, j, u)
                    tiles.append(b)
            else:
                for h in range(1 if job[0] == "w1" else 2):
                    b = ps.tile([P, 2, 256], F32, name="tp", tag="tp", bufs=4)
                    for u in range(2):
                        for jj in range(2):
                            tr(b[:, u, P * jj : P * (jj + 1)], job, 2 * h + jj, u)
                    tiles.append(b)
            bank[job] = tiles
            if job in srt:
                srt.pop(job)
            else:
                free_raw(job)

        def copy_half(job, h, dst, engine):
            copy(engine, dst[:, 256 * h : 256 * (h + 1), :], bank[job][h][:].rearrange("p u r -> p r u"))

        def affine(i, engines):
            g = i % NG
            tiles = bank.pop(("wv", i))
            a = sb.tile([P, 4, CH], BF16, name="at", tag="at", bufs=3)
            for u in range(2):
                bv = tiles[u][:].bitcast(BF16).rearrange("p (r e) -> p r e", e=2)
                for e in range(2):
                    t = 2 * u + e
                    col = 4 * g + t
                    if engines[u] == "s":
                        nc.scalar.activation(out=a[:, t, :], in_=bv[:, :, e], func=ACT.Identity,
                                             bias=dwb[:, col : col + 1], scale=dww[:, col : col + 1])
                    else:
                        nc.vector.tensor_scalar(out=a[:, t, :], in0=bv[:, :, e],
                                                scalar1=dww[:, col : col + 1], scalar2=dwb[:, col : col + 1],
                                                op0=ALU.mult, op1=ALU.add)
            at[i] = a

        def interleave_a(i, lo, hi, engine):
            o = grp[i][:, lo:hi, :]
            a = at[i][:, :, lo:hi].rearrange("p t c -> p c t")
            if engine == "g":
                nc.gpsimd.tensor_scalar(out=o, in0=a, scalar1=1.0, scalar2=0.0, op0=ALU.mult, op1=ALU.add)
            else:
                copy(engine, o, a)

        def new_early_group(i):
            g = sb.tile([P, CH, 4], BF16, name="ag2", tag="ag2", bufs=3, align_bytes=64)
            grp[i] = g

        def interleave_a_gpsimd(i):
            g = sb.tile([P, CH, 4], BF16, name="ag", tag="ag", bufs=1, align_bytes=64)
            grp[i] = g
            for q in range(4):
                interleave_a(i, P * q, P * (q + 1), "g")
            at.pop(i)

        def q_a(i):
            g = grp.pop(i)
            cd = sb.tile([P, CH], U32, name="ac", tag="ac", bufs=9, align_bytes=256)
            sc = sb.tile([P, CH], U8, name="asc", tag="asc", bufs=9, align_bytes=256)
            nc.vector.quantize_mx(out=cd[:].bitcast(FP8X4), scales=sc[:], in_=g[:].rearrange("p c t -> p (c t)"))
            a_codes[i] = cd
            a_scales[i] = sc

        def c_x(i, h, engine):
            if h == 0:
                d = sb.tile([P, CH, 2], F32, name="xt", tag="xt", bufs=3)
                xt[i] = d
            copy_half(("x", i), h, xt[i], engine)
            if h == 1:
                bank.pop(("x", i))

        def c_w(job, engines):
            d = sb.tile([P, R if job[0] == "w1" else 512, 2], F32, name="srt", tag="srt", bufs=SRT_BUFS, align_bytes=64)
            for h in range(len(bank[job])):
                copy_half(job, h, d, engines[h])
            bank.pop(job)
            grp[job] = d

        def q_w(job):
            d = grp.pop(job)
            i = d[:].rearrange("p c u -> p (c u)").bitcast(BF16)
            if job[0] == "w1":
                nc.vector.quantize_mx(out=w1_codes[:, job[1], :].bitcast(FP8X4), scales=w1_scales[:, job[1], :], in_=i)
            else:
                nc.vector.quantize_mx(out=w_codes[job[1]][:, job[2], :].bitcast(FP8X4),
                                      scales=w_scales[job[1]][:, job[2], :], in_=i)

        def m1_pass(acc, s, t, gk):
            c = s // NG
            G = s % NG
            cols = slice(P * t, P * (t + 1))
            nc.tensor.matmul_mx(out=acc[:],
                                lhsT=w_codes[G][:, gk, cols].bitcast(FP8X4), lhsT_scale=w_scales[G][:, gk, cols],
                                rhs=a_codes[NG * c + gk][:].bitcast(FP8X4), rhs_scale=a_scales[NG * c + gk][:],
                                start=(gk == 0), stop=(gk == NG - 1))

        def y_add(acc, s, t):
            c = s // NG
            G = s % NG
            if t == 0:
                y = sb.tile([P, 4, CH], BF16, name="yt", tag="yt", bufs=2)
                yt[s] = y
            xv = xt[s][:].rearrange("p r u -> p (r u)").bitcast(BF16).rearrange("p (r t) -> p r t", t=4)
            col = 4 * G + t
            nc.vector.scalar_tensor_tensor(out=yt[s][:, t, :], in0=acc[:], scalar=pwb[:, col : col + 1],
                                           in1=xv[:, :, t], op0=ALU.add, op1=ALU.add)
            if t == 3:
                xt.pop(s)
                if G == NG - 1:
                    for gk in range(NG):
                        a_codes.pop(NG * c + gk)
                        a_scales.pop(NG * c + gk)

        def m1_y(s, t):
            acc = ps.tile([P, CH], F32, name="s1", tag="s1", bufs=4)
            for gk in range(NG):
                m1_pass(acc, s, t, gk)
            y_add(acc, s, t)

        def i_y(s, lo, hi):
            if lo == 0:
                g = sb.tile([P, CH, 4], BF16, name="yg", tag="yg", bufs=2, align_bytes=64)
                grp[("y", s)] = g
            nc.vector.tensor_copy(out=grp[("y", s)][:, lo:hi, :], in_=yt[s][:, :, lo:hi].rearrange("p t c -> p c t"))
            if hi == CH:
                yt.pop(s)

        def q_y(s, lo, hi):
            if lo == 0:
                cd = sb.tile([P, CH], U32, name="yc", tag="yc", bufs=6, align_bytes=256)
                sc = sb.tile([P, CH], U8, name="ysc", tag="ysc", bufs=6, align_bytes=256)
                y_codes[s] = cd
                y_scales[s] = sc
            nc.vector.quantize_mx(out=y_codes[s][:, lo:hi].bitcast(FP8X4), scales=y_scales[s][:, lo:hi],
                                  in_=grp[("y", s)][:, lo:hi, :].rearrange("p c t -> p (c t)"))
            if hi == CH:
                grp.pop(("y", s))

        def m2_pass(acc, c, j, G):
            cols = slice(P * j, P * (j + 1))
            nc.tensor.matmul_mx(out=acc,
                                lhsT=y_codes[NG * c + G][:, cols].bitcast(FP8X4),
                                lhsT_scale=y_scales[NG * c + G][:, cols],
                                rhs=w1_codes[:, G, :].bitcast(FP8X4), rhs_scale=w1_scales[:, G, :],
                                start=(G == 0), stop=(G == NG - 1))

        def m2(c, h):
            acc = ps.tile([P, 2, R], F32, name="s1", tag="s1", bufs=4)
            for jj in range(2):
                for G in range(NG):
                    m2_pass(acc[:, jj, :], c, 2 * h + jj, G)
            bank[("o", c, h)] = acc
            if h == 1:
                for G in range(NG):
                    y_codes.pop(NG * c + G)
                    y_scales.pop(NG * c + G)

        def out_rows(c, h):
            return out_f[CH * c + 256 * h : CH * c + 256 * (h + 1), :].rearrange("(jj p) r -> p jj r", p=P)

        def store(c, h):
            acc = bank.pop(("o", c, h))
            ob = sb.tile([P, 2, R], F32, name="ob", tag="ob", bufs=3)
            nc.scalar.copy(out=ob[:], in_=acc[:])
            nc.scalar.dma_start(out=out_rows(c, h), in_=ob[:])

        prefetch()
        acc0 = []
        for t in range(4):
            acc0.append(ps.tile([P, CH], F32, name="s1", tag="s1", bufs=4))
        for i in range(NG):
            transposes(("wv", i))
            transposes(("w", 0, i))
            prefetch()
            affine(i, ("s", "v"))
            c_w(("w", 0, i), ("s", "v"))
            new_early_group(i)
            interleave_a(i, 0, 256, "s")
            interleave_a(i, 256, 384, "g")
            interleave_a(i, 384, 512, "g")
            at.pop(i)
            if i >= 2:
                for t in range(4):
                    m1_pass(acc0[t], 0, t, i - 2)
            q_w(("w", 0, i))
            if i >= 1:
                q_a(i - 1)
        transposes(("x", 0))
        prefetch()
        for t in range(4):
            m1_pass(acc0[t], 0, t, NG - 2)
        c_x(0, 0, "s")
        q_a(NG - 1)
        c_x(0, 1, "v")
        for t in range(4):
            m1_pass(acc0[t], 0, t, NG - 1)

        early_q = {}
        gpsimd_ia = {}
        steady_q = {}
        for i in range(NG, STEPS):
            ts = t_step[("wv", i)]
            if i < 8:
                early_q[ts + 1] = early_q.get(ts + 1, []) + [i]
            else:
                gpsimd_ia[ts + 1] = gpsimd_ia.get(ts + 1, []) + [i]
                steady_q[ts + 2] = steady_q.get(ts + 2, []) + [i]

        pending_q = []

        def do_run(run, extra):
            for job in run:
                transposes(job)
            prefetch()
            for job in run:
                if job[0] == "x":
                    c_x(job[1], 0, "s")
            for job in run:
                if job[0] == "wv":
                    affine(job[1], ("s", "v") if extra else ("s", "s"))
                    if job[1] < 8:
                        new_early_group(job[1])
                        interleave_a(job[1], 0, 256, "s")
                elif job[0] == "w" or job[0] == "w1":
                    c_w(job, ("s", "v") if t_step[job] == 0 else ("s", "s"))
                    pending_q.append(job)

        def flush_q():
            while len(pending_q) > 0:
                q_w(pending_q.pop(0))

        for s in range(STEPS):
            c = s // NG
            G = s % NG
            if c >= 1 and G == 1:
                store(c - 1, 0)
            if c >= 1 and G == 2:
                store(c - 1, 1)
            step_runs = runs[s]
            do_run(step_runs[0], False)
            if s + SORT_AHEAD >= FIRST_SORTED_STEP and s + SORT_AHEAD < STEPS:
                for job in reversed(runs[s + SORT_AHEAD][0]):
                    sort_words(job, "s")
                prefetch()
            if s >= 1:
                i_y(s - 1, 0, CH)
            if s + 1 < STEPS:
                c_x(s + 1, 1, "v")
            if s >= 1:
                q_y(s - 1, 0, CH)
            for i in early_q.get(s, []):
                interleave_a(i, 256, 512, "v")
                at.pop(i)
            for i in early_q.get(s, []):
                q_a(i)
            for i in steady_q.get(s, []):
                q_a(i)
            for i in gpsimd_ia.get(s, []):
                interleave_a_gpsimd(i)
            for t in range(4):
                if s == 0:
                    y_add(acc0[t], 0, t)
                else:
                    m1_y(s, t)
                if t >= 2:
                    flush_q()
                if t >= 1 and len(step_runs) > t:
                    do_run(step_runs[t], t == 3)
            if s == 0:
                while len(acc0) > 0:
                    acc0.pop()
            if c >= 1 and G == 0:
                m2(c - 1, 0)
            if c >= 1 and G == 1:
                m2(c - 1, 1)

        c = NCH - 1
        accs = []
        for j in range(4):
            accs.append(ps.tile([P, R], F32, name="tp", tag="tp", bufs=4))
            for G in range(NG - 1):
                m2_pass(accs[j][:], c, j, G)
        for h in range(2):
            i_y(STEPS - 1, 256 * h, 256 * (h + 1))
            q_y(STEPS - 1, 256 * h, 256 * (h + 1))
        for h in range(2):
            ob = sb.tile([P, 2, R], F32, name="ob", tag="ob", bufs=3)
            for jj in range(2):
                m2_pass(accs[2 * h + jj][:], c, 2 * h + jj, NG - 1)
                copy("s" if h == 0 else "v", ob[:, jj, :], accs[2 * h + jj][:])
            if h == 0:
                nc.scalar.dma_start(out=out_rows(c, h), in_=ob[:])
            else:
                nc.sync.dma_start(out=out_rows(c, h), in_=ob[:])
